import numpy as np
import ml_dtypes


def mxq(x, axis, fmt="e4m3"):
    dtype, down = {"e4m3": (ml_dtypes.float8_e4m3fn, 7), "e5m2": (ml_dtypes.float8_e5m2, 14)}[fmt]
    v = np.moveaxis(np.asarray(x, np.float32).astype(ml_dtypes.bfloat16).astype(np.float64), axis, -1)
    blocks = v.reshape(v.shape[:-1] + (-1, 32))
    amax = np.abs(blocks).max(-1, keepdims=True)
    byte = np.maximum(np.where(amax > 0, np.frexp(amax)[1] - 1 + 127, 0) - down, 1)
    scale = np.exp2(byte - 127.0)
    codes = (blocks / scale).astype(np.float32).astype(dtype).astype(np.float64)
    return np.moveaxis((codes * scale).reshape(v.shape), -1, axis)


WIDE = False


def mx_kscale(k):
    if not WIDE:
        return np.ones(k)
    levels = np.array([20, -20, 10, -10, 0])
    a = np.random.permutation(np.resize(levels, k // 512 * 4)).reshape(k // 512, 4)
    idx = np.arange(k)
    return np.exp2(a[idx // 512, idx % 128 // 32])


BF16 = ml_dtypes.bfloat16


def bf(x):
    return np.asarray(x, np.float32).astype(BF16)


def f64(x):
    return np.asarray(x).astype(np.float64)


B, I, J, K, D = 512, 1024, 1024, 4, 2
EPS = 1e-8


def caps_sum(xf, ws):
    return (xf.transpose(2, 0, 1) @ ws.transpose(2, 1, 0)).transpose(1, 2, 0)


def setup_inputs():
    u = mx_kscale(I)
    c = 2.0 / np.sqrt(J * D * (K * K / 4.0 + K / 12.0))
    X = bf(np.random.standard_normal((B, J, D)))
    w0 = bf(np.random.random((I, J, K, D)) * c)
    g = bf(np.random.standard_normal((B, I, D)) * np.exp2(np.random.randint(-12, 1, (B, 1, 1))) * 32.0 * u[None, :, None])
    s = caps_sum(f64(X), f64(w0).sum(axis=2))
    return {"X": X, "weight": bf(f64(w0) / u[:, None, None, None]),
            "s": np.asarray(s, np.float32), "grad_out": g}


def reference(X, weight, s, grad_out):
    sf = f64(s)
    g = f64(grad_out)
    n2 = np.sum(sf * sf, axis=-1, keepdims=True)
    n = np.sqrt(n2)
    f = n2 / (1.0 + n2) / (n + EPS)
    c = 2.0 / ((1.0 + n2) ** 2 * (n + EPS)) - n / ((1.0 + n2) * (n + EPS) ** 2)
    p = np.sum(g * sf, axis=-1, keepdims=True)
    ds = f * g + c * p * sf
    dq = mxq(ds, 1, "e5m2")
    wq = mxq(f64(weight).sum(axis=2), 0, "e4m3")
    gx = dq.transpose(2, 0, 1) @ wq.transpose(2, 0, 1)
    return gx.transpose(1, 2, 0)

@@ -1,0 +1,231 @@
+import concourse.mybir as mybir
+from concourse.masks import make_identity
+
+F32 = mybir.dt.float32
+BF16 = mybir.dt.bfloat16
+U32 = mybir.dt.uint32
+U8 = mybir.dt.uint8
+I32 = mybir.dt.int32
+E4M3_X4 = mybir.dt.float8_e4m3fn_x4
+E5M2_X4 = mybir.dt.float8_e5m2_x4
+ACT = mybir.ActivationFunctionType
+ALU = mybir.AluOpType
+
+B, I, J, K, D = 512, 1024, 1024, 4, 2
+EPS = 1e-8
+
+P = 128
+PACK = 4
+K_PASS = P * PACK
+PASSES = I // K_PASS
+TOKEN_TILES = B // P
+J_CHUNK = 256
+J_CHUNKS = J // J_CHUNK
+W_CHUNKS = J_CHUNKS * PASSES
+W_SLOT = 3 * J_CHUNK
+
+FLOPS = 2 * B * I * J * D
+BYTES = 2 * I * J * K * D + 4 * B * I * D + 2 * B * I * D + 4 * B * J * D
+
+
+def tile_primary_capsule_t_v_kernel(tc, X, weight, s, grad_out, out):
+    nc = tc.nc
+    s_rows = s.rearrange("(n p) i d -> n p i d", p=P)
+    g_rows = grad_out.rearrange("(n p) i d -> n p i d", p=P)
+    out_rows = out.rearrange("(n p) j d -> n p j d", p=P)
+    w_rows = weight.rearrange("(c t p) j k d -> c p t j (k d)", t=PACK, p=P)
+
+    with tc.tile_pool(name="sb", bufs=1) as sb, tc.psum_pool(name="ps", bufs=1) as ps, tc.manual_schedule():
+        eps_col = sb.tile([P, 1], F32)
+        nc.vector.memset(eps_col[:], EPS)
+        one_col = sb.tile([P, 1], F32)
+        nc.vector.memset(one_col[:], 1.0)
+        ident = sb.tile([P, P], F32)
+        make_identity(nc, ident[:])
+
+        ds_codes = sb.tile([P, TOKEN_TILES, PASSES * D * P], U32, align_bytes=64)
+        ds_scales = sb.tile([P, TOKEN_TILES, PASSES * D * P], U8, align_bytes=64)
+        w_codes = sb.tile([P, W_CHUNKS, W_SLOT], U32, align_bytes=64)
+        w_scales = sb.tile([P, W_CHUNKS, W_SLOT], U8, align_bytes=64)
+        nc.vector.memset(w_codes[:, :, J_CHUNK : 2 * J_CHUNK].bitcast(I32), 0)
+        nc.vector.memset(w_scales[:, :, J_CHUNK : 2 * J_CHUNK].bitcast(I32), 0)
+
+        tokens = {}
+        w_tiles = {}
+        banks = {}
+
+        def load_tokens(n):
+            s_sb = sb.tile([P, I, D], F32, tag="s", bufs=2)
+            nc.sync.dma_start(out=s_sb[:], in_=s_rows[n])
+            g_sb = sb.tile([P, I, D], BF16, tag="g", bufs=2)
+            nc.sync.dma_start(out=g_sb[:], in_=g_rows[n])
+            tokens[n] = {"s": s_sb, "g": g_sb}
+
+        def load_weights(w):
+            jc, c = divmod(w, PASSES)
+            w_sb = sb.tile([P, PACK, J_CHUNK, K * D], BF16, tag="w", bufs=3)
+            nc.sync.dma_start(out=w_sb[:], in_=w_rows[c][:, :, jc * J_CHUNK : (jc + 1) * J_CHUNK, :])
+            w_tiles[w] = w_sb
+
+        def dots(n):
+            t = tokens[n]
+            sq = sb.tile([P, I, D], F32, tag="sq")
+            nc.scalar.activation(out=sq[:], in_=t["s"][:], func=ACT.Square)
+            gs = sb.tile([P, I, D], F32, tag="gs")
+            nc.vector.tensor_tensor(out=gs[:], in0=t["g"][:], in1=t["s"][:], op=ALU.mult)
+            p_dot = sb.tile([P, I], F32, tag="p_dot", bufs=2)
+            nc.vector.tensor_tensor(out=p_dot[:], in0=gs[:, :, 0], in1=gs[:, :, 1], op=ALU.add)
+            n2 = sb.tile([P, I], F32, tag="n2", bufs=2)
+            nc.vector.tensor_tensor(out=n2[:], in0=sq[:, :, 0], in1=sq[:, :, 1], op=ALU.add)
+            t["p"] = p_dot
+            t["n2"] = n2
+
+        def reciprocals(n):
+            t = tokens[n]
+            r = sb.tile([P, I], F32, tag="r", bufs=2)
+            a = sb.tile([P, I], F32, tag="a")
+            m = sb.tile([P, I], F32, tag="m")
+            nc.scalar.activation(out=r[:], in_=t["n2"][:], func=ACT.Sqrt)
+            nc.scalar.activation(out=a[:], in_=t["n2"][:], func=ACT.Square, bias=one_col[:])
+            nc.scalar.activation(out=r[:], in_=r[:], func=ACT.Square, bias=eps_col[:])
+            nc.scalar.activation(out=a[:], in_=a[:], func=ACT.Abs_reciprocal_sqrt)
+            nc.scalar.activation(out=r[:], in_=r[:], func=ACT.Abs_reciprocal_sqrt)
+            nc.scalar.activation(out=m[:], in_=r[:], func=ACT.Identity, scale=-EPS, bias=one_col[:])
+            t["r"] = r
+            t["a"] = a
+            t["m"] = m
+
+        def two_terms(n):
+            t = tokens[n]
+            ar = sb.tile([P, I], F32, tag="ar")
+            nc.vector.tensor_tensor(out=ar[:], in0=t["a"][:], in1=t["r"][:], op=ALU.mult)
+            c_fac = t["m"]
+            nc.vector.scalar_tensor_tensor(
+                out=c_fac[:], in0=t["a"][:], scalar=2.0, in1=t["m"][:], op0=ALU.mult, op1=ALU.subtract
+            )
+            nc.vector.tensor_tensor(out=c_fac[:], in0=c_fac[:], in1=ar[:], op=ALU.mult)
+            f_fac = ar
+            nc.vector.tensor_tensor(out=f_fac[:], in0=ar[:], in1=t["n2"][:], op=ALU.mult)
+            h_fac = t["p"]
+            nc.vector.tensor_tensor(out=h_fac[:], in0=t["p"][:], in1=c_fac[:], op=ALU.mult)
+            fg = sb.tile([P, D, I], F32, tag="fg")
+            nc.vector.tensor_tensor(
+                out=fg[:],
+                in0=f_fac[:].unsqueeze(1).to_broadcast([P, D, I]),
+                in1=t["g"][:].rearrange("p i d -> p d i"),
+                op=ALU.mult,
+            )
+            hs = sb.tile([P, D, I], F32, tag="hs")
+            nc.vector.tensor_tensor(
+                out=hs[:],
+                in0=h_fac[:].unsqueeze(1).to_broadcast([P, D, I]),
+                in1=t["s"][:].rearrange("p i d -> p d i"),
+                op=ALU.mult,
+            )
+            t["fg"] = fg
+            t["hs"] = hs
+
+        def turn(n):
+            t = tokens[n]
+            ds_bf = sb.tile([P, PASSES, D, P, PACK], BF16, tag="ds_bf", bufs=2, align_bytes=64)
+            for c in range(PASSES):
+                for d in range(D):
+                    turned = ps.tile([P, PACK, P], F32, tag="turned", bufs=2)
+                    for k in range(PACK):
+                        i_cols = slice((c * PACK + k) * P, (c * PACK + k + 1) * P)
+                        nc.tensor.matmul(
+                            out=turned[:, k, :], lhsT=t["fg"][:, d, i_cols], rhs=ident[:],
+                            is_transpose=True, start=True, stop=False,
+                        )
+                        nc.tensor.matmul(
+                            out=turned[:, k, :], lhsT=t["hs"][:, d, i_cols], rhs=ident[:],
+                            is_transpose=True, start=False, stop=True,
+                        )
+                    nc.scalar.copy(out=ds_bf[:, c, d, :, :], in_=turned[:].rearrange("p t b -> p b t"))
+            t["ds_bf"] = ds_bf
+
+        def quantise_tokens(n):
+            nc.vector.quantize_mx(
+                out=ds_codes[:, n, :].bitcast(E5M2_X4),
+                scales=ds_scales[:, n, :],
+                in_=tokens[n]["ds_bf"][:].rearrange("p c d b t -> p (c d b t)"),
+            )
+
+        def sum_weights(w):
+            w_sb = w_tiles[w]
+            half = sb.tile([P, J_CHUNK, PACK, 2 * D], F32, tag="half")
+            nc.vector.tensor_tensor(
+                out=half[:].rearrange("p j t e -> p t j e"),
+                in0=w_sb[:, :, :, 0 : 2 * D],
+                in1=w_sb[:, :, :, 2 * D : 4 * D],
+                op=ALU.add,
+            )
+            ws_bf = sb.tile([P, D, J_CHUNK, PACK], BF16, tag="ws_bf", bufs=2, align_bytes=64)
+            nc.vector.tensor_tensor(
+                out=ws_bf[:],
+                in0=half[:, :, :, 0:D].rearrange("p j t d -> p d j t"),
+                in1=half[:, :, :, D : 2 * D].rearrange("p j t d -> p d j t"),
+                op=ALU.add,
+            )
+            for d in range(D):
+                cols = slice(2 * d * J_CHUNK, (2 * d + 1) * J_CHUNK)
+                nc.vector.quantize_mx(
+                    out=w_codes[:, w, cols].bitcast(E4M3_X4),
+                    scales=w_scales[:, w, cols],
+                    in_=ws_bf[:, d, :, :].rearrange("p j t -> p (j t)"),
+                )
+
+        def multiply(w):
+            jc, c = divmod(w, PASSES)
+            for n in range(TOKEN_TILES):
+                if c == 0:
+                    bank = ps.tile([P, D, J_CHUNK], F32, tag="bank", bufs=6)
+                    banks[n] = bank
+                for d in range(D):
+                    ds_cols = slice((c * D + d) * P, (c * D + d + 1) * P)
+                    w_cols = slice(d * J_CHUNK, (d + 2) * J_CHUNK)
+                    nc.tensor.matmul_mx(
+                        out=banks[n][:].rearrange("p d j -> p (d j)"),
+                        lhsT=ds_codes[:, n, ds_cols].bitcast(E5M2_X4),
+                        lhsT_scale=ds_scales[:, n, ds_cols],
+                        rhs=w_codes[:, w, w_cols].bitcast(E4M3_X4),
+                        rhs_scale=w_scales[:, w, w_cols],
+                        start=(c == 0 and d == 0),
+                        stop=(c == PASSES - 1 and d == D - 1),
+                    )
+            if c == PASSES - 1:
+                for n in range(TOKEN_TILES):
+                    result = sb.tile([P, J_CHUNK, D], F32, tag="result", bufs=4)
+                    nc.scalar.copy(out=result[:], in_=banks[n][:].rearrange("p d j -> p j d"))
+                    nc.sync.dma_start(
+                        out=out_rows[n][:, jc * J_CHUNK : (jc + 1) * J_CHUNK, :], in_=result[:]
+                    )
+
+        load_tokens(0)
+        load_weights(0)
+        load_tokens(1)
+        load_weights(1)
+        load_weights(2)
+        dots(0)
+        reciprocals(0)
+        for n in range(TOKEN_TILES):
+            sum_weights(n)
+            if n + 1 < TOKEN_TILES:
+                dots(n + 1)
+                reciprocals(n + 1)
+            two_terms(n)
+            turn(n)
+            if n >= 1:
+                quantise_tokens(n - 1)
+            if n + 2 < TOKEN_TILES:
+                load_tokens(n + 2)
+            load_weights(n + 3)
+        for w in range(TOKEN_TILES, W_CHUNKS):
+            sum_weights(w)
+            if w + 3 < W_CHUNKS:
+                load_weights(w + 3)
+            if w == TOKEN_TILES:
+                quantise_tokens(TOKEN_TILES - 1)
+                for early in range(TOKEN_TILES):
+                    multiply(early)
+            multiply(w)

@@ -52,33 +52,40 @@ def tile_primary_capsule_t_v_kernel(tc, X, weight, s, grad_out, out):
 
         tokens = {}
         w_tiles = {}
+        halves = {}
+        sums = {}
         banks = {}
 
         def load_tokens(n):
-            s_sb = sb.tile([P, I, D], F32, tag="s", bufs=2)
+            s_sb = sb.tile([P, I, D], F32, tag="s", bufs=3)
             nc.sync.dma_start(out=s_sb[:], in_=s_rows[n])
-            g_sb = sb.tile([P, I, D], BF16, tag="g", bufs=2)
+            g_sb = sb.tile([P, I, D], BF16, tag="g", bufs=3)
             nc.sync.dma_start(out=g_sb[:], in_=g_rows[n])
             tokens[n] = {"s": s_sb, "g": g_sb}
 
         def load_weights(w):
             jc, c = divmod(w, PASSES)
-            w_sb = sb.tile([P, PACK, J_CHUNK, K * D], BF16, tag="w", bufs=3)
+            w_sb = sb.tile([P, PACK, J_CHUNK, K * D], BF16, tag="w", bufs=2)
             nc.sync.dma_start(out=w_sb[:], in_=w_rows[c][:, :, jc * J_CHUNK : (jc + 1) * J_CHUNK, :])
             w_tiles[w] = w_sb
 
-        def dots(n):
+        def token_products(n):
             t = tokens[n]
             sq = sb.tile([P, I, D], F32, tag="sq")
             nc.scalar.activation(out=sq[:], in_=t["s"][:], func=ACT.Square)
             gs = sb.tile([P, I, D], F32, tag="gs")
             nc.vector.tensor_tensor(out=gs[:], in0=t["g"][:], in1=t["s"][:], op=ALU.mult)
-            p_dot = sb.tile([P, I], F32, tag="p_dot", bufs=2)
-            nc.vector.tensor_tensor(out=p_dot[:], in0=gs[:, :, 0], in1=gs[:, :, 1], op=ALU.add)
+            t["sq"] = sq
+            t["gs"] = gs
+
+        def token_sums(n):
+            t = tokens[n]
             n2 = sb.tile([P, I], F32, tag="n2", bufs=2)
-            nc.vector.tensor_tensor(out=n2[:], in0=sq[:, :, 0], in1=sq[:, :, 1], op=ALU.add)
-            t["p"] = p_dot
+            nc.vector.tensor_tensor(out=n2[:], in0=t["sq"][:, :, 0], in1=t["sq"][:, :, 1], op=ALU.add)
+            p_dot = sb.tile([P, I], F32, tag="p_dot", bufs=2)
+            nc.vector.tensor_tensor(out=p_dot[:], in0=t["gs"][:, :, 0], in1=t["gs"][:, :, 1], op=ALU.add)
             t["n2"] = n2
+            t["p"] = p_dot
 
         def reciprocals(n):
             t = tokens[n]
@@ -95,7 +102,7 @@ def tile_primary_capsule_t_v_kernel(tc, X, weight, s, grad_out, out):
             t["a"] = a
             t["m"] = m
 
-        def two_terms(n):
+        def factors(n):
             t = tokens[n]
             ar = sb.tile([P, I], F32, tag="ar")
             nc.vector.tensor_tensor(out=ar[:], in0=t["a"][:], in1=t["r"][:], op=ALU.mult)
@@ -103,31 +110,40 @@ def tile_primary_capsule_t_v_kernel(tc, X, weight, s, grad_out, out):
             nc.vector.scalar_tensor_tensor(
                 out=c_fac[:], in0=t["a"][:], scalar=2.0, in1=t["m"][:], op0=ALU.mult, op1=ALU.subtract
             )
-            nc.vector.tensor_tensor(out=c_fac[:], in0=c_fac[:], in1=ar[:], op=ALU.mult)
-            f_fac = ar
+            f_fac = sb.tile([P, I], F32, tag="f_fac")
             nc.vector.tensor_tensor(out=f_fac[:], in0=ar[:], in1=t["n2"][:], op=ALU.mult)
-            h_fac = t["p"]
-            nc.vector.tensor_tensor(out=h_fac[:], in0=t["p"][:], in1=c_fac[:], op=ALU.mult)
+            nc.vector.tensor_tensor(out=c_fac[:], in0=c_fac[:], in1=ar[:], op=ALU.mult)
+            t["f"] = f_fac
+            t["c"] = c_fac
+
+        def first_term(n):
+            t = tokens[n]
             fg = sb.tile([P, D, I], F32, tag="fg")
             nc.vector.tensor_tensor(
                 out=fg[:],
-                in0=f_fac[:].unsqueeze(1).to_broadcast([P, D, I]),
+                in0=t["f"][:].unsqueeze(1).to_broadcast([P, D, I]),
                 in1=t["g"][:].rearrange("p i d -> p d i"),
                 op=ALU.mult,
             )
+            h_fac = t["p"]
+            nc.vector.tensor_tensor(out=h_fac[:], in0=t["p"][:], in1=t["c"][:], op=ALU.mult)
+            t["fg"] = fg
+            t["h"] = h_fac
+
+        def second_term(n):
+            t = tokens[n]
             hs = sb.tile([P, D, I], F32, tag="hs")
             nc.vector.tensor_tensor(
                 out=hs[:],
-                in0=h_fac[:].unsqueeze(1).to_broadcast([P, D, I]),
+                in0=t["h"][:].unsqueeze(1).to_broadcast([P, D, I]),
                 in1=t["s"][:].rearrange("p i d -> p d i"),
                 op=ALU.mult,
             )
-            t["fg"] = fg
             t["hs"] = hs
 
         def turn(n):
             t = tokens[n]
-            ds_bf = sb.tile([P, PASSES, D, P, PACK], BF16, tag="ds_bf", bufs=2, align_bytes=64)
+            ds_bf = sb.tile([P, PASSES, D, P, PACK], BF16, tag="ds_bf", align_bytes=64)
             for c in range(PASSES):
                 for d in range(D):
                     turned = ps.tile([P, PACK, P], F32, tag="turned", bufs=2)
@@ -151,15 +167,19 @@ def tile_primary_capsule_t_v_kernel(tc, X, weight, s, grad_out, out):
                 in_=tokens[n]["ds_bf"][:].rearrange("p c d b t -> p (c d b t)"),
             )
 
-        def sum_weights(w):
+        def weights_first_add(w):
             w_sb = w_tiles[w]
-            half = sb.tile([P, J_CHUNK, PACK, 2 * D], F32, tag="half")
+            half = sb.tile([P, J_CHUNK, PACK, 2 * D], F32, tag="half", bufs=2)
             nc.vector.tensor_tensor(
                 out=half[:].rearrange("p j t e -> p t j e"),
                 in0=w_sb[:, :, :, 0 : 2 * D],
                 in1=w_sb[:, :, :, 2 * D : 4 * D],
                 op=ALU.add,
             )
+            halves[w] = half
+
+        def weights_second_add(w):
+            half = halves[w]
             ws_bf = sb.tile([P, D, J_CHUNK, PACK], BF16, tag="ws_bf", bufs=2, align_bytes=64)
             nc.vector.tensor_tensor(
                 out=ws_bf[:],
@@ -167,12 +187,15 @@ def tile_primary_capsule_t_v_kernel(tc, X, weight, s, grad_out, out):
                 in1=half[:, :, :, D : 2 * D].rearrange("p j t d -> p d j t"),
                 op=ALU.add,
             )
+            sums[w] = ws_bf
+
+        def weights_quantise(w):
             for d in range(D):
                 cols = slice(2 * d * J_CHUNK, (2 * d + 1) * J_CHUNK)
                 nc.vector.quantize_mx(
                     out=w_codes[:, w, cols].bitcast(E4M3_X4),
                     scales=w_scales[:, w, cols],
-                    in_=ws_bf[:, d, :, :].rearrange("p j t -> p (j t)"),
+                    in_=sums[w][:, d, :, :].rearrange("p j t -> p (j t)"),
                 )
 
         def multiply(w):
@@ -195,9 +218,9 @@ def tile_primary_capsule_t_v_kernel(tc, X, weight, s, grad_out, out):
                     )
             if c == PASSES - 1:
                 for n in range(TOKEN_TILES):
-                    result = sb.tile([P, J_CHUNK, D], F32, tag="result", bufs=4)
+                    result = sb.tile([P, J_CHUNK, D], F32, tag="result", bufs=3)
                     nc.scalar.copy(out=result[:], in_=banks[n][:].rearrange("p d j -> p j d"))
-                    nc.sync.dma_start(
+                    nc.scalar.dma_start(
                         out=out_rows[n][:, jc * J_CHUNK : (jc + 1) * J_CHUNK, :], in_=result[:]
                     )
 
@@ -205,27 +228,39 @@ def tile_primary_capsule_t_v_kernel(tc, X, weight, s, grad_out, out):
         load_weights(0)
         load_tokens(1)
         load_weights(1)
-        load_weights(2)
-        dots(0)
+        load_tokens(2)
+        token_products(0)
+        token_sums(0)
         reciprocals(0)
         for n in range(TOKEN_TILES):
-            sum_weights(n)
-            if n + 1 < TOKEN_TILES:
-                dots(n + 1)
+            following = n + 1 < TOKEN_TILES
+            weights_first_add(n)
+            load_weights(n + 2)
+            if following:
+                token_products(n + 1)
+            weights_second_add(n)
+            if following:
+                token_sums(n + 1)
                 reciprocals(n + 1)
-            two_terms(n)
-            turn(n)
+            weights_quantise(n)
+            factors(n)
+            first_term(n)
             if n >= 1:
                 quantise_tokens(n - 1)
-            if n + 2 < TOKEN_TILES:
-                load_tokens(n + 2)
-            load_weights(n + 3)
+            second_term(n)
+            turn(n)
+            if n + 3 < TOKEN_TILES:
+                load_tokens(n + 3)
+        weights_first_add(TOKEN_TILES)
+        load_weights(TOKEN_TILES + 2)
+        quantise_tokens(TOKEN_TILES - 1)
+        for early in range(TOKEN_TILES):
+            multiply(early)
         for w in range(TOKEN_TILES, W_CHUNKS):
-            sum_weights(w)
+            weights_second_add(w)
+            if w + 1 < W_CHUNKS:
+                weights_first_add(w + 1)
             if w + 3 < W_CHUNKS:
                 load_weights(w + 3)
-            if w == TOKEN_TILES:
-                quantise_tokens(TOKEN_TILES - 1)
-                for early in range(TOKEN_TILES):
-                    multiply(early)
+            weights_quantise(w)
             multiply(w)

@@ -23,6 +23,11 @@ J_CHUNK = 256
 J_CHUNKS = J // J_CHUNK
 W_CHUNKS = J_CHUNKS * PASSES
 W_SLOT = 3 * J_CHUNK
+TENSOR_J_GROUP = 64
+TENSOR_J = 3 * TENSOR_J_GROUP
+LEAD = 1
+ROUND_CHUNKS = LEAD + TOKEN_TILES
+TENSOR_CHUNK = ROUND_CHUNKS
 
 FLOPS = 2 * B * I * J * D
 BYTES = 2 * I * J * K * D + 4 * B * I * D + 2 * B * I * D + 4 * B * J * D
@@ -42,6 +47,8 @@ def tile_primary_capsule_t_v_kernel(tc, X, weight, s, grad_out, out):
         nc.vector.memset(one_col[:], 1.0)
         ident = sb.tile([P, P], F32)
         make_identity(nc, ident[:])
+        ident_bf = sb.tile([P, P], BF16)
+        make_identity(nc, ident_bf[:])
 
         ds_codes = sb.tile([P, TOKEN_TILES, PASSES * D * P], U32, align_bytes=64)
         ds_scales = sb.tile([P, TOKEN_TILES, PASSES * D * P], U8, align_bytes=64)
@@ -51,10 +58,10 @@ def tile_primary_capsule_t_v_kernel(tc, X, weight, s, grad_out, out):
         nc.vector.memset(w_scales[:, :, J_CHUNK : 2 * J_CHUNK].bitcast(I32), 0)
 
         tokens = {}
-        w_tiles = {}
-        halves = {}
-        sums = {}
+        weights = {}
         banks = {}
+        ready_tiles = []
+        ready_chunks = []
 
         def load_tokens(n):
             s_sb = sb.tile([P, I, D], F32, tag="s", bufs=3)
@@ -67,33 +74,34 @@ def tile_primary_capsule_t_v_kernel(tc, X, weight, s, grad_out, out):
             jc, c = divmod(w, PASSES)
             w_sb = sb.tile([P, PACK, J_CHUNK, K * D], BF16, tag="w", bufs=2)
             nc.sync.dma_start(out=w_sb[:], in_=w_rows[c][:, :, jc * J_CHUNK : (jc + 1) * J_CHUNK, :])
-            w_tiles[w] = w_sb
+            weights[w] = {"w": w_sb}
+
+        def token_squares(n):
+            t = tokens[n]
+            prod = sb.tile([P, 2, I, D], F32, tag="prod")
+            nc.scalar.activation(out=prod[:, 0, :, :], in_=t["s"][:], func=ACT.Square)
+            t["prod"] = prod
 
         def token_products(n):
             t = tokens[n]
-            sq = sb.tile([P, I, D], F32, tag="sq")
-            nc.scalar.activation(out=sq[:], in_=t["s"][:], func=ACT.Square)
-            gs = sb.tile([P, I, D], F32, tag="gs")
-            nc.vector.tensor_tensor(out=gs[:], in0=t["g"][:], in1=t["s"][:], op=ALU.mult)
-            t["sq"] = sq
-            t["gs"] = gs
+            nc.vector.tensor_tensor(out=t["prod"][:, 1, :, :], in0=t["g"][:], in1=t["s"][:], op=ALU.mult)
 
         def token_sums(n):
             t = tokens[n]
-            n2 = sb.tile([P, I], F32, tag="n2", bufs=2)
-            nc.vector.tensor_tensor(out=n2[:], in0=t["sq"][:, :, 0], in1=t["sq"][:, :, 1], op=ALU.add)
-            p_dot = sb.tile([P, I], F32, tag="p_dot", bufs=2)
-            nc.vector.tensor_tensor(out=p_dot[:], in0=t["gs"][:, :, 0], in1=t["gs"][:, :, 1], op=ALU.add)
-            t["n2"] = n2
-            t["p"] = p_dot
+            dots = sb.tile([P, 2, I], F32, tag="dots", bufs=2)
+            nc.vector.tensor_tensor(
+                out=dots[:], in0=t["prod"][:, :, :, 0], in1=t["prod"][:, :, :, 1], op=ALU.add
+            )
+            t["dots"] = dots
 
         def reciprocals(n):
             t = tokens[n]
-            r = sb.tile([P, I], F32, tag="r", bufs=2)
+            n2 = t["dots"][:, 0, :]
+            r = sb.tile([P, I], F32, tag="r")
             a = sb.tile([P, I], F32, tag="a")
             m = sb.tile([P, I], F32, tag="m")
-            nc.scalar.activation(out=r[:], in_=t["n2"][:], func=ACT.Sqrt)
-            nc.scalar.activation(out=a[:], in_=t["n2"][:], func=ACT.Square, bias=one_col[:])
+            nc.scalar.activation(out=r[:], in_=n2, func=ACT.Sqrt)
+            nc.scalar.activation(out=a[:], in_=n2, func=ACT.Square, bias=one_col[:])
             nc.scalar.activation(out=r[:], in_=r[:], func=ACT.Square, bias=eps_col[:])
             nc.scalar.activation(out=a[:], in_=a[:], func=ACT.Abs_reciprocal_sqrt)
             nc.scalar.activation(out=r[:], in_=r[:], func=ACT.Abs_reciprocal_sqrt)
@@ -102,51 +110,40 @@ def tile_primary_capsule_t_v_kernel(tc, X, weight, s, grad_out, out):
             t["a"] = a
             t["m"] = m
 
+        def factor_parts(n):
+            t = tokens[n]
+            nc.vector.scalar_tensor_tensor(
+                out=t["m"][:], in0=t["a"][:], scalar=2.0, in1=t["m"][:], op0=ALU.mult, op1=ALU.subtract
+            )
+            facs = sb.tile([P, 2, I], F32, tag="facs")
+            nc.vector.tensor_tensor(out=facs[:, 0, :], in0=t["a"][:], in1=t["r"][:], op=ALU.mult)
+            t["facs"] = facs
+
+        def factor_c(n):
+            t = tokens[n]
+            nc.vector.tensor_tensor(out=t["facs"][:, 1, :], in0=t["facs"][:, 0, :], in1=t["m"][:], op=ALU.mult)
+
         def factors(n):
             t = tokens[n]
-            ar = sb.tile([P, I], F32, tag="ar")
-            nc.vector.tensor_tensor(out=ar[:], in0=t["a"][:], in1=t["r"][:], op=ALU.mult)
-            c_fac = t["m"]
-            nc.vector.scalar_tensor_tensor(
-                out=c_fac[:], in0=t["a"][:], scalar=2.0, in1=t["m"][:], op0=ALU.mult, op1=ALU.subtract
-            )
-            f_fac = sb.tile([P, I], F32, tag="f_fac")
-            nc.vector.tensor_tensor(out=f_fac[:], in0=ar[:], in1=t["n2"][:], op=ALU.mult)
-            nc.vector.tensor_tensor(out=c_fac[:], in0=c_fac[:], in1=ar[:], op=ALU.mult)
-            t["f"] = f_fac
-            t["c"] = c_fac
+            nc.vector.tensor_tensor(out=t["dots"][:], in0=t["dots"][:], in1=t["facs"][:], op=ALU.mult)
 
-        def first_term(n):
+        def term(n, which, name, source):
             t = tokens[n]
-            fg = sb.tile([P, D, I], F32, tag="fg")
+            planes = sb.tile([P, D, I], F32, tag=name)
             nc.vector.tensor_tensor(
-                out=fg[:],
-                in0=t["f"][:].unsqueeze(1).to_broadcast([P, D, I]),
-                in1=t["g"][:].rearrange("p i d -> p d i"),
+                out=planes[:],
+                in0=t["dots"][:, which, :].unsqueeze(1).to_broadcast([P, D, I]),
+                in1=t[source][:].rearrange("p i d -> p d i"),
                 op=ALU.mult,
             )
-            h_fac = t["p"]
-            nc.vector.tensor_tensor(out=h_fac[:], in0=t["p"][:], in1=t["c"][:], op=ALU.mult)
-            t["fg"] = fg
-            t["h"] = h_fac
-
-        def second_term(n):
-            t = tokens[n]
-            hs = sb.tile([P, D, I], F32, tag="hs")
-            nc.vector.tensor_tensor(
-                out=hs[:],
-                in0=t["h"][:].unsqueeze(1).to_broadcast([P, D, I]),
-                in1=t["s"][:].rearrange("p i d -> p d i"),
-                op=ALU.mult,
-            )
-            t["hs"] = hs
+            t[name] = planes
 
         def turn(n):
             t = tokens[n]
             ds_bf = sb.tile([P, PASSES, D, P, PACK], BF16, tag="ds_bf", align_bytes=64)
             for c in range(PASSES):
                 for d in range(D):
-                    turned = ps.tile([P, PACK, P], F32, tag="turned", bufs=2)
+                    turned = ps.tile([P, PACK, P], F32, tag="small", bufs=2)
                     for k in range(PACK):
                         i_cols = slice((c * PACK + k) * P, (c * PACK + k + 1) * P)
                         nc.tensor.matmul(
@@ -167,40 +164,54 @@ def tile_primary_capsule_t_v_kernel(tc, X, weight, s, grad_out, out):
                 in_=tokens[n]["ds_bf"][:].rearrange("p c d b t -> p (c d b t)"),
             )
 
+        def first_j(w):
+            return TENSOR_J if w == TENSOR_CHUNK else 0
+
         def weights_first_add(w):
-            w_sb = w_tiles[w]
+            t = weights[w]
             half = sb.tile([P, J_CHUNK, PACK, 2 * D], F32, tag="half", bufs=2)
             nc.vector.tensor_tensor(
-                out=half[:].rearrange("p j t e -> p t j e"),
-                in0=w_sb[:, :, :, 0 : 2 * D],
-                in1=w_sb[:, :, :, 2 * D : 4 * D],
+                out=half[:, first_j(w) :, :, :].rearrange("p j t e -> p t j e"),
+                in0=t["w"][:, :, first_j(w) :, 0 : 2 * D],
+                in1=t["w"][:, :, first_j(w) :, 2 * D : 4 * D],
                 op=ALU.add,
             )
-            halves[w] = half
+            ws_bf = sb.tile([P, D, J_CHUNK, PACK], BF16, tag="ws_bf", bufs=2, align_bytes=64)
+            t["half"] = half
+            t["ws_bf"] = ws_bf
 
         def weights_second_add(w):
-            half = halves[w]
-            ws_bf = sb.tile([P, D, J_CHUNK, PACK], BF16, tag="ws_bf", bufs=2, align_bytes=64)
+            t = weights[w]
             nc.vector.tensor_tensor(
-                out=ws_bf[:],
-                in0=half[:, :, :, 0:D].rearrange("p j t d -> p d j t"),
-                in1=half[:, :, :, D : 2 * D].rearrange("p j t d -> p d j t"),
+                out=t["ws_bf"][:, :, first_j(w) :, :],
+                in0=t["half"][:, first_j(w) :, :, 0:D].rearrange("p j t d -> p d j t"),
+                in1=t["half"][:, first_j(w) :, :, D : 2 * D].rearrange("p j t d -> p d j t"),
                 op=ALU.add,
             )
-            sums[w] = ws_bf
 
-        def weights_quantise(w):
-            for d in range(D):
-                cols = slice(2 * d * J_CHUNK, (2 * d + 1) * J_CHUNK)
-                nc.vector.quantize_mx(
-                    out=w_codes[:, w, cols].bitcast(E4M3_X4),
-                    scales=w_scales[:, w, cols],
-                    in_=sums[w][:, d, :, :].rearrange("p j t -> p (j t)"),
-                )
+        def weights_tensor_sum(w):
+            t = weights[w]
+            for j0 in range(0, first_j(w), TENSOR_J_GROUP):
+                j_cols = slice(j0, j0 + TENSOR_J_GROUP)
+                summed = ps.tile([P, PACK, TENSOR_J_GROUP, D], F32, tag="small", bufs=2)
+                for k in range(K):
+                    nc.tensor.matmul(
+                        out=summed[:], lhsT=ident_bf[:], rhs=t["w"][:, :, j_cols, k * D : (k + 1) * D],
+                        start=(k == 0), stop=(k == K - 1),
+                    )
+                nc.scalar.copy(out=t["ws_bf"][:, :, j_cols, :], in_=summed[:].rearrange("p t j d -> p d j t"))
 
-        def multiply(w):
+        def weights_quantise(w, d):
+            cols = slice(2 * d * J_CHUNK, (2 * d + 1) * J_CHUNK)
+            nc.vector.quantize_mx(
+                out=w_codes[:, w, cols].bitcast(E4M3_X4),
+                scales=w_scales[:, w, cols],
+                in_=weights[w]["ws_bf"][:, d, :, :].rearrange("p j t -> p (j t)"),
+            )
+
+        def multiply(w, tiles):
             jc, c = divmod(w, PASSES)
-            for n in range(TOKEN_TILES):
+            for n in tiles:
                 if c == 0:
                     bank = ps.tile([P, D, J_CHUNK], F32, tag="bank", bufs=6)
                     banks[n] = bank
@@ -217,50 +228,79 @@ def tile_primary_capsule_t_v_kernel(tc, X, weight, s, grad_out, out):
                         stop=(c == PASSES - 1 and d == D - 1),
                     )
             if c == PASSES - 1:
-                for n in range(TOKEN_TILES):
+                for n in tiles:
                     result = sb.tile([P, J_CHUNK, D], F32, tag="result", bufs=3)
-                    nc.scalar.copy(out=result[:], in_=banks[n][:].rearrange("p d j -> p j d"))
-                    nc.scalar.dma_start(
-                        out=out_rows[n][:, jc * J_CHUNK : (jc + 1) * J_CHUNK, :], in_=result[:]
-                    )
+                    out_cols = out_rows[n][:, jc * J_CHUNK : (jc + 1) * J_CHUNK, :]
+                    if jc == J_CHUNKS - 1 and n % 2 == 1:
+                        nc.vector.tensor_copy(out=result[:], in_=banks[n][:].rearrange("p d j -> p j d"))
+                        nc.sync.dma_start(out=out_cols, in_=result[:])
+                    else:
+                        nc.scalar.copy(out=result[:], in_=banks[n][:].rearrange("p d j -> p j d"))
+                        nc.scalar.dma_start(out=out_cols, in_=result[:])
+
+        def chunk_ready(w):
+            multiply(w, ready_tiles)
+            ready_chunks.append(w)
+
+        def tile_ready(n):
+            for w in ready_chunks:
+                multiply(w, [n])
+            ready_tiles.append(n)
 
         load_tokens(0)
         load_weights(0)
         load_tokens(1)
         load_weights(1)
         load_tokens(2)
+        token_squares(0)
         token_products(0)
         token_sums(0)
         reciprocals(0)
+        token_squares(1)
+        for w in range(LEAD):
+            weights_first_add(w)
+            load_weights(w + 2)
+            weights_second_add(w)
+            weights_quantise(w, 0)
+            weights_quantise(w, 1)
+            chunk_ready(w)
         for n in range(TOKEN_TILES):
-            following = n + 1 < TOKEN_TILES
-            weights_first_add(n)
-            load_weights(n + 2)
-            if following:
+            w = LEAD + n
+            weights_first_add(w)
+            load_weights(w + 2)
+            if n + 1 < TOKEN_TILES:
                 token_products(n + 1)
-            weights_second_add(n)
-            if following:
+            weights_second_add(w)
+            if n + 1 < TOKEN_TILES:
                 token_sums(n + 1)
                 reciprocals(n + 1)
-            weights_quantise(n)
+            if n + 2 < TOKEN_TILES:
+                token_squares(n + 2)
+            factor_parts(n)
+            weights_quantise(w, 0)
+            factor_c(n)
+            weights_quantise(w, 1)
+            chunk_ready(w)
             factors(n)
-            first_term(n)
             if n >= 1:
                 quantise_tokens(n - 1)
-            second_term(n)
+                tile_ready(n - 1)
+            if n == TOKEN_TILES - 1:
+                weights_first_add(TENSOR_CHUNK)
+                load_weights(TENSOR_CHUNK + 2)
+                weights_tensor_sum(TENSOR_CHUNK)
+            term(n, 0, "fg", "g")
+            term(n, 1, "hs", "s")
             turn(n)
             if n + 3 < TOKEN_TILES:
                 load_tokens(n + 3)
-        weights_first_add(TOKEN_TILES)
-        load_weights(TOKEN_TILES + 2)
-        quantise_tokens(TOKEN_TILES - 1)
-        for early in range(TOKEN_TILES):
-            multiply(early)
-        for w in range(TOKEN_TILES, W_CHUNKS):
+        for w in range(ROUND_CHUNKS, W_CHUNKS):
             weights_second_add(w)
             if w + 1 < W_CHUNKS:
                 weights_first_add(w + 1)
-            if w + 3 < W_CHUNKS:
-                load_weights(w + 3)
-            weights_quantise(w)
-            multiply(w)
+            weights_quantise(w, 0)
+            weights_quantise(w, 1)
+            chunk_ready(w)
+            if w == ROUND_CHUNKS:
+                quantise_tokens(TOKEN_TILES - 1)
+                tile_ready(TOKEN_TILES - 1)

@@ -183,9 +183,9 @@ def tile_primary_capsule_t_v_kernel(tc, X, weight, s, grad_out, out):
         def weights_second_add(w):
             t = weights[w]
             nc.vector.tensor_tensor(
-                out=t["ws_bf"][:, :, first_j(w) :, :],
-                in0=t["half"][:, first_j(w) :, :, 0:D].rearrange("p j t d -> p d j t"),
-                in1=t["half"][:, first_j(w) :, :, D : 2 * D].rearrange("p j t d -> p d j t"),
+                out=t["ws_bf"][:, :, first_j(w) :, :].rearrange("p d j t -> p j t d"),
+                in0=t["half"][:, first_j(w) :, :, 0:D],
+                in1=t["half"][:, first_j(w) :, :, D : 2 * D],
                 op=ALU.add,
             )
 

@@ -28,6 +28,9 @@ TENSOR_J = 3 * TENSOR_J_GROUP
 LEAD = 1
 ROUND_CHUNKS = LEAD + TOKEN_TILES
 TENSOR_CHUNK = ROUND_CHUNKS
+TURNED_CHUNKS = ROUND_CHUNKS
+J_GROUP = P // D
+J_GROUPS = J_CHUNK // J_GROUP
 
 FLOPS = 2 * B * I * J * D
 BYTES = 2 * I * J * K * D + 4 * B * I * D + 2 * B * I * D + 4 * B * J * D
@@ -143,7 +146,7 @@ def tile_primary_capsule_t_v_kernel(tc, X, weight, s, grad_out, out):
             ds_bf = sb.tile([P, PASSES, D, P, PACK], BF16, tag="ds_bf", align_bytes=64)
             for c in range(PASSES):
                 for d in range(D):
-                    turned = ps.tile([P, PACK, P], F32, tag="small", bufs=2)
+                    turned = ps.tile([P, PACK, P], F32, tag="tp", bufs=4)
                     for k in range(PACK):
                         i_cols = slice((c * PACK + k) * P, (c * PACK + k + 1) * P)
                         nc.tensor.matmul(
@@ -189,11 +192,74 @@ def tile_primary_capsule_t_v_kernel(tc, X, weight, s, grad_out, out):
                 op=ALU.add,
             )
 
+        def weights_first_add_planes(w):
+            t = weights[w]
+            planes = sb.tile([P, 2, PACK * J_CHUNK, D], F32, tag="half", bufs=2)
+            rows = t["w"][:].rearrange("p t j e -> p (t j) e")
+            nc.vector.tensor_tensor(
+                out=planes[:].rearrange("p h x d -> p x h d"),
+                in0=rows[:, :, 0 : 2 * D].rearrange("p x (h d) -> p x h d", d=D),
+                in1=rows[:, :, 2 * D : 4 * D].rearrange("p x (h d) -> p x h d", d=D),
+                op=ALU.add,
+            )
+            ws_bf = sb.tile([P, D, J_CHUNK, PACK], BF16, tag="ws_bf", bufs=2, align_bytes=64)
+            t["planes"] = planes
+            t["ws_bf"] = ws_bf
+
+        def weights_turned_sum(w):
+            t = weights[w]
+            forward_banks = {}
+            rounded_tiles = {}
+            back_banks = {}
+
+            def forward(g):
+                bank = ps.tile([P, PACK, P], F32, tag="tp", bufs=4)
+                for k in range(PACK):
+                    x0 = k * J_CHUNK + g * J_GROUP
+                    for h in range(2):
+                        nc.tensor.matmul(
+                            out=bank[:, k, :],
+                            lhsT=t["planes"][:, h, x0 : x0 + J_GROUP, :].rearrange("p x d -> p (x d)"),
+                            rhs=ident[:], is_transpose=True, start=(h == 0), stop=(h == 1),
+                        )
+                forward_banks[g] = bank
+
+            def rounded(g):
+                mid = sb.tile([P, 2, P, 2], BF16, tag="mid", bufs=3, align_bytes=64)
+                nc.scalar.copy(out=mid[:], in_=forward_banks[g][:].rearrange("q (u e) p -> q u p e", e=2))
+                rounded_tiles[g] = mid
+
+            def back(g):
+                if g % 2 == 0:
+                    pair = ps.tile([P, 2, 2, P], F32, tag="tp", bufs=4)
+                    back_banks[g // 2] = pair
+                words = rounded_tiles[g][:].rearrange("q u p e -> q (u p e)").bitcast(F32)
+                for u in range(2):
+                    nc.tensor.transpose(
+                        out=back_banks[g // 2][:, u, g % 2, :], in_=words[:, u * P : (u + 1) * P], identity=ident[:]
+                    )
+
+            def placed(pair):
+                j_cols = slice(pair * 2 * J_GROUP, (pair + 1) * 2 * J_GROUP)
+                nc.scalar.copy(
+                    out=t["ws_bf"][:].bitcast(F32)[:, :, j_cols, :],
+                    in_=back_banks[pair][:].rearrange("p u g (j d) -> p d (g j) u", d=D),
+                )
+
+            forward(0)
+            for g in range(J_GROUPS):
+                if g + 1 < J_GROUPS:
+                    forward(g + 1)
+                rounded(g)
+                back(g)
+                if g % 2 == 1:
+                    placed(g // 2)
+
         def weights_tensor_sum(w):
             t = weights[w]
             for j0 in range(0, first_j(w), TENSOR_J_GROUP):
                 j_cols = slice(j0, j0 + TENSOR_J_GROUP)
-                summed = ps.tile([P, PACK, TENSOR_J_GROUP, D], F32, tag="small", bufs=2)
+                summed = ps.tile([P, PACK, TENSOR_J_GROUP, D], F32, tag="tp", bufs=4)
                 for k in range(K):
                     nc.tensor.matmul(
                         out=summed[:], lhsT=ident_bf[:], rhs=t["w"][:, :, j_cols, k * D : (k + 1) * D],
@@ -213,7 +279,7 @@ def tile_primary_capsule_t_v_kernel(tc, X, weight, s, grad_out, out):
             jc, c = divmod(w, PASSES)
             for n in tiles:
                 if c == 0:
-                    bank = ps.tile([P, D, J_CHUNK], F32, tag="bank", bufs=6)
+                    bank = ps.tile([P, D, J_CHUNK], F32, tag="bank", bufs=4)
                     banks[n] = bank
                 for d in range(D):
                     ds_cols = slice((c * D + d) * P, (c * D + d + 1) * P)
@@ -258,33 +324,30 @@ def tile_primary_capsule_t_v_kernel(tc, X, weight, s, grad_out, out):
         reciprocals(0)
         token_squares(1)
         for w in range(LEAD):
-            weights_first_add(w)
+            weights_first_add_planes(w)
             load_weights(w + 2)
-            weights_second_add(w)
-            weights_quantise(w, 0)
-            weights_quantise(w, 1)
-            chunk_ready(w)
+            weights_turned_sum(w)
         for n in range(TOKEN_TILES):
             w = LEAD + n
-            weights_first_add(w)
-            load_weights(w + 2)
             if n + 1 < TOKEN_TILES:
                 token_products(n + 1)
-            weights_second_add(w)
+            weights_first_add_planes(w)
+            load_weights(w + 2)
+            weights_turned_sum(w)
             if n + 1 < TOKEN_TILES:
                 token_sums(n + 1)
                 reciprocals(n + 1)
             if n + 2 < TOKEN_TILES:
                 token_squares(n + 2)
             factor_parts(n)
-            weights_quantise(w, 0)
-            factor_c(n)
-            weights_quantise(w, 1)
-            chunk_ready(w)
-            factors(n)
             if n >= 1:
                 quantise_tokens(n - 1)
                 tile_ready(n - 1)
+            factor_c(n)
+            weights_quantise(w - 1, 0)
+            factors(n)
+            weights_quantise(w - 1, 1)
+            chunk_ready(w - 1)
             if n == TOKEN_TILES - 1:
                 weights_first_add(TENSOR_CHUNK)
                 load_weights(TENSOR_CHUNK + 2)
@@ -296,6 +359,10 @@ def tile_primary_capsule_t_v_kernel(tc, X, weight, s, grad_out, out):
                 load_tokens(n + 3)
         for w in range(ROUND_CHUNKS, W_CHUNKS):
             weights_second_add(w)
+            if w == ROUND_CHUNKS:
+                weights_quantise(w - 1, 0)
+                weights_quantise(w - 1, 1)
+                chunk_ready(w - 1)
             if w + 1 < W_CHUNKS:
                 weights_first_add(w + 1)
             weights_quantise(w, 0)

@@ -100,35 +100,37 @@ def tile_primary_capsule_t_v_kernel(tc, X, weight, s, grad_out, out):
         def reciprocals(n):
             t = tokens[n]
             n2 = t["dots"][:, 0, :]
-            r = sb.tile([P, I], F32, tag="r")
-            a = sb.tile([P, I], F32, tag="a")
-            m = sb.tile([P, I], F32, tag="m")
+            r = sb.tile([P, I], F32, tag="r", bufs=2)
+            a2 = sb.tile([P, I], F32, tag="a2", bufs=2)
             nc.scalar.activation(out=r[:], in_=n2, func=ACT.Sqrt)
-            nc.scalar.activation(out=a[:], in_=n2, func=ACT.Square, bias=one_col[:])
+            nc.scalar.activation(out=a2[:], in_=n2, func=ACT.Square, bias=one_col[:])
             nc.scalar.activation(out=r[:], in_=r[:], func=ACT.Square, bias=eps_col[:])
-            nc.scalar.activation(out=a[:], in_=a[:], func=ACT.Abs_reciprocal_sqrt)
+            nc.scalar.activation(out=a2[:], in_=a2[:], func=ACT.Abs_reciprocal_sqrt, scale=0.25)
             nc.scalar.activation(out=r[:], in_=r[:], func=ACT.Abs_reciprocal_sqrt)
-            nc.scalar.activation(out=m[:], in_=r[:], func=ACT.Identity, scale=-EPS, bias=one_col[:])
             t["r"] = r
-            t["a"] = a
-            t["m"] = m
+            t["a2"] = a2
 
         def factor_parts(n):
             t = tokens[n]
-            nc.vector.scalar_tensor_tensor(
-                out=t["m"][:], in0=t["a"][:], scalar=2.0, in1=t["m"][:], op0=ALU.mult, op1=ALU.subtract
-            )
             facs = sb.tile([P, 2, I], F32, tag="facs")
-            nc.vector.tensor_tensor(out=facs[:, 0, :], in0=t["a"][:], in1=t["r"][:], op=ALU.mult)
+            nc.vector.tensor_tensor(out=facs[:, 0, :], in0=t["a2"][:], in1=t["r"][:], op=ALU.mult)
+            nc.vector.scalar_tensor_tensor(
+                out=t["r"][:], in0=t["r"][:], scalar=EPS, in1=t["a2"][:], op0=ALU.mult, op1=ALU.add
+            )
             t["facs"] = facs
 
         def factor_c(n):
             t = tokens[n]
-            nc.vector.tensor_tensor(out=t["facs"][:, 1, :], in0=t["facs"][:, 0, :], in1=t["m"][:], op=ALU.mult)
+            nc.vector.scalar_tensor_tensor(
+                out=t["facs"][:, 1, :], in0=t["r"][:], scalar=1.0, in1=t["facs"][:, 0, :],
+                op0=ALU.subtract, op1=ALU.mult,
+            )
 
         def factors(n):
             t = tokens[n]
-            nc.vector.tensor_tensor(out=t["dots"][:], in0=t["dots"][:], in1=t["facs"][:], op=ALU.mult)
+            nc.vector.scalar_tensor_tensor(
+                out=t["dots"][:], in0=t["dots"][:], scalar=0.5, in1=t["facs"][:], op0=ALU.mult, op1=ALU.mult
+            )
 
         def term(n, which, name, source):
             t = tokens[n]
@@ -141,9 +143,9 @@ def tile_primary_capsule_t_v_kernel(tc, X, weight, s, grad_out, out):
             )
             t[name] = planes
 
-        def turn(n):
+        def turn_transposes(n):
             t = tokens[n]
-            ds_bf = sb.tile([P, PASSES, D, P, PACK], BF16, tag="ds_bf", align_bytes=64)
+            t["turned"] = []
             for c in range(PASSES):
                 for d in range(D):
                     turned = ps.tile([P, PACK, P], F32, tag="tp", bufs=4)
@@ -157,7 +159,16 @@ def tile_primary_capsule_t_v_kernel(tc, X, weight, s, grad_out, out):
                             out=turned[:, k, :], lhsT=t["hs"][:, d, i_cols], rhs=ident[:],
                             is_transpose=True, start=False, stop=True,
                         )
-                    nc.scalar.copy(out=ds_bf[:, c, d, :, :], in_=turned[:].rearrange("p t b -> p b t"))
+                    t["turned"].append(turned)
+
+        def turn_copies(n):
+            t = tokens[n]
+            ds_bf = sb.tile([P, PASSES, D, P, PACK], BF16, tag="ds_bf", align_bytes=64)
+            for c in range(PASSES):
+                for d in range(D):
+                    nc.scalar.copy(
+                        out=ds_bf[:, c, d, :, :], in_=t["turned"][c * D + d][:].rearrange("p t b -> p b t")
+                    )
             t["ds_bf"] = ds_bf
 
         def quantise_tokens(n):
@@ -206,13 +217,13 @@ def tile_primary_capsule_t_v_kernel(tc, X, weight, s, grad_out, out):
             t["planes"] = planes
             t["ws_bf"] = ws_bf
 
-        def weights_turned_sum(w):
-            t = weights[w]
-            forward_banks = {}
-            rounded_tiles = {}
-            back_banks = {}
+        def weights_turned_sum_note():
+            pass
 
-            def forward(g):
+        def weights_forward(w):
+            t = weights[w]
+            t["forward"] = []
+            for g in range(J_GROUPS):
                 bank = ps.tile([P, PACK, P], F32, tag="tp", bufs=4)
                 for k in range(PACK):
                     x0 = k * J_CHUNK + g * J_GROUP
@@ -222,38 +233,37 @@ def tile_primary_capsule_t_v_kernel(tc, X, weight, s, grad_out, out):
                             lhsT=t["planes"][:, h, x0 : x0 + J_GROUP, :].rearrange("p x d -> p (x d)"),
                             rhs=ident[:], is_transpose=True, start=(h == 0), stop=(h == 1),
                         )
-                forward_banks[g] = bank
+                t["forward"].append(bank)
 
-            def rounded(g):
-                mid = sb.tile([P, 2, P, 2], BF16, tag="mid", bufs=3, align_bytes=64)
-                nc.scalar.copy(out=mid[:], in_=forward_banks[g][:].rearrange("q (u e) p -> q u p e", e=2))
-                rounded_tiles[g] = mid
+        def weights_rounded(w):
+            t = weights[w]
+            t["rounded"] = []
+            for g in range(J_GROUPS):
+                mid = sb.tile([P, 2, P, 2], BF16, tag="mid", bufs=4, align_bytes=64)
+                nc.scalar.copy(out=mid[:], in_=t["forward"][g][:].rearrange("q (u e) p -> q u p e", e=2))
+                t["rounded"].append(mid)
 
-            def back(g):
-                if g % 2 == 0:
-                    pair = ps.tile([P, 2, 2, P], F32, tag="tp", bufs=4)
-                    back_banks[g // 2] = pair
-                words = rounded_tiles[g][:].rearrange("q u p e -> q (u p e)").bitcast(F32)
-                for u in range(2):
-                    nc.tensor.transpose(
-                        out=back_banks[g // 2][:, u, g % 2, :], in_=words[:, u * P : (u + 1) * P], identity=ident[:]
-                    )
+        def weights_back(w):
+            t = weights[w]
+            t["back"] = []
+            for pair in range(J_GROUPS // 2):
+                bank = ps.tile([P, 2, 2, P], F32, tag="tp", bufs=4)
+                for g in range(2):
+                    words = t["rounded"][2 * pair + g][:].rearrange("q u p e -> q (u p e)").bitcast(F32)
+                    for u in range(2):
+                        nc.tensor.transpose(
+                            out=bank[:, u, g, :], in_=words[:, u * P : (u + 1) * P], identity=ident[:]
+                        )
+                t["back"].append(bank)
 
-            def placed(pair):
+        def weights_placed(w):
+            t = weights[w]
+            for pair in range(J_GROUPS // 2):
                 j_cols = slice(pair * 2 * J_GROUP, (pair + 1) * 2 * J_GROUP)
                 nc.scalar.copy(
                     out=t["ws_bf"][:].bitcast(F32)[:, :, j_cols, :],
-                    in_=back_banks[pair][:].rearrange("p u g (j d) -> p d (g j) u", d=D),
+                    in_=t["back"][pair][:].rearrange("p u g (j d) -> p d (g j) u", d=D),
                 )
-
-            forward(0)
-            for g in range(J_GROUPS):
-                if g + 1 < J_GROUPS:
-                    forward(g + 1)
-                rounded(g)
-                back(g)
-                if g % 2 == 1:
-                    placed(g // 2)
 
         def weights_tensor_sum(w):
             t = weights[w]
@@ -326,37 +336,47 @@ def tile_primary_capsule_t_v_kernel(tc, X, weight, s, grad_out, out):
         for w in range(LEAD):
             weights_first_add_planes(w)
             load_weights(w + 2)
-            weights_turned_sum(w)
+            weights_forward(w)
+            weights_rounded(w)
+            weights_back(w)
+            weights_placed(w)
+        token_products(1)
         for n in range(TOKEN_TILES):
             w = LEAD + n
             if n + 1 < TOKEN_TILES:
-                token_products(n + 1)
-            weights_first_add_planes(w)
-            load_weights(w + 2)
-            weights_turned_sum(w)
-            if n + 1 < TOKEN_TILES:
                 token_sums(n + 1)
                 reciprocals(n + 1)
+            if n >= 1:
+                turn_copies(n - 1)
+            factor_parts(n)
             if n + 2 < TOKEN_TILES:
                 token_squares(n + 2)
-            factor_parts(n)
-            if n >= 1:
-                quantise_tokens(n - 1)
-                tile_ready(n - 1)
+            weights_first_add_planes(w)
+            load_weights(w + 2)
+            weights_forward(w)
             factor_c(n)
             weights_quantise(w - 1, 0)
             factors(n)
             weights_quantise(w - 1, 1)
+            weights_rounded(w)
             chunk_ready(w - 1)
+            weights_back(w)
+            term(n, 0, "fg", "g")
+            weights_placed(w)
+            if n >= 1:
+                quantise_tokens(n - 1)
+                tile_ready(n - 1)
             if n == TOKEN_TILES - 1:
                 weights_first_add(TENSOR_CHUNK)
                 load_weights(TENSOR_CHUNK + 2)
                 weights_tensor_sum(TENSOR_CHUNK)
-            term(n, 0, "fg", "g")
             term(n, 1, "hs", "s")
-            turn(n)
+            turn_transposes(n)
+            if n + 2 < TOKEN_TILES:
+                token_products(n + 2)
             if n + 3 < TOKEN_TILES:
                 load_tokens(n + 3)
+        turn_copies(TOKEN_TILES - 1)
         for w in range(ROUND_CHUNKS, W_CHUNKS):
             weights_second_add(w)
             if w == ROUND_CHUNKS:

@@ -305,7 +305,7 @@ def tile_primary_capsule_t_v_kernel(tc, X, weight, s, grad_out, out):
                     )
             if c == PASSES - 1:
                 for n in tiles:
-                    result = sb.tile([P, J_CHUNK, D], F32, tag="result", bufs=3)
+                    result = sb.tile([P, J_CHUNK, D], F32, tag="result", bufs=4)
                     out_cols = out_rows[n][:, jc * J_CHUNK : (jc + 1) * J_CHUNK, :]
                     if jc == J_CHUNKS - 1 and n % 2 == 1:
                         nc.vector.tensor_copy(out=result[:], in_=banks[n][:].rearrange("p d j -> p j d"))
@@ -343,26 +343,31 @@ def tile_primary_capsule_t_v_kernel(tc, X, weight, s, grad_out, out):
         token_products(1)
         for n in range(TOKEN_TILES):
             w = LEAD + n
+            if n >= 1:
+                turn_copies(n - 1)
+            if n == 0:
+                weights_first_add_planes(w)
+                load_weights(w + 2)
+                weights_forward(w)
             if n + 1 < TOKEN_TILES:
                 token_sums(n + 1)
                 reciprocals(n + 1)
-            if n >= 1:
-                turn_copies(n - 1)
             factor_parts(n)
             if n + 2 < TOKEN_TILES:
                 token_squares(n + 2)
-            weights_first_add_planes(w)
-            load_weights(w + 2)
-            weights_forward(w)
+            if n >= 1:
+                weights_first_add_planes(w)
+                load_weights(w + 2)
+                weights_forward(w)
             factor_c(n)
             weights_quantise(w - 1, 0)
             factors(n)
             weights_quantise(w - 1, 1)
             weights_rounded(w)
-            chunk_ready(w - 1)
             weights_back(w)
-            term(n, 0, "fg", "g")
             weights_placed(w)
+            chunk_ready(w - 1)
+            term(n, 0, "fg", "g")
             if n >= 1:
                 quantise_tokens(n - 1)
                 tile_ready(n - 1)
@@ -383,11 +388,11 @@ def tile_primary_capsule_t_v_kernel(tc, X, weight, s, grad_out, out):
                 weights_quantise(w - 1, 0)
                 weights_quantise(w - 1, 1)
                 chunk_ready(w - 1)
+            if w == ROUND_CHUNKS + 1:
+                quantise_tokens(TOKEN_TILES - 1)
+                tile_ready(TOKEN_TILES - 1)
             if w + 1 < W_CHUNKS:
                 weights_first_add(w + 1)
             weights_quantise(w, 0)
             weights_quantise(w, 1)
             chunk_ready(w)
-            if w == ROUND_CHUNKS:
-                quantise_tokens(TOKEN_TILES - 1)
-                tile_ready(TOKEN_TILES - 1)

@@ -102,8 +102,10 @@ def tile_primary_capsule_t_v_kernel(tc, X, weight, s, grad_out, out):
             n2 = t["dots"][:, 0, :]
             r = sb.tile([P, I], F32, tag="r", bufs=2)
             a2 = sb.tile([P, I], F32, tag="a2", bufs=2)
-            nc.scalar.activation(out=r[:], in_=n2, func=ACT.Sqrt)
+            nc.scalar.activation(out=r[:], in_=n2, func=ACT.Abs_reciprocal_sqrt)
             nc.scalar.activation(out=a2[:], in_=n2, func=ACT.Square, bias=one_col[:])
+            nc.scalar.activation(out=r[:], in_=r[:], func=ACT.Square)
+            nc.scalar.activation(out=r[:], in_=r[:], func=ACT.Abs_reciprocal_sqrt)
             nc.scalar.activation(out=r[:], in_=r[:], func=ACT.Square, bias=eps_col[:])
             nc.scalar.activation(out=a2[:], in_=a2[:], func=ACT.Abs_reciprocal_sqrt, scale=0.25)
             nc.scalar.activation(out=r[:], in_=r[:], func=ACT.Abs_reciprocal_sqrt)

import concourse.mybir as mybir
from concourse.masks import make_identity

F32 = mybir.dt.float32
BF16 = mybir.dt.bfloat16
U32 = mybir.dt.uint32
U8 = mybir.dt.uint8
I32 = mybir.dt.int32
E4M3_X4 = mybir.dt.float8_e4m3fn_x4
E5M2_X4 = mybir.dt.float8_e5m2_x4
ACT = mybir.ActivationFunctionType
ALU = mybir.AluOpType

B, I, J, K, D = 512, 1024, 1024, 4, 2
EPS = 1e-8

P = 128
PACK = 4
K_PASS = P * PACK
PASSES = I // K_PASS
TOKEN_TILES = B // P
J_CHUNK = 256
J_CHUNKS = J // J_CHUNK
W_CHUNKS = J_CHUNKS * PASSES
W_SLOT = 3 * J_CHUNK
TENSOR_J_GROUP = 64
TENSOR_J = 3 * TENSOR_J_GROUP
LEAD = 1
ROUND_CHUNKS = LEAD + TOKEN_TILES
TENSOR_CHUNK = ROUND_CHUNKS
TURNED_CHUNKS = ROUND_CHUNKS
J_GROUP = P // D
J_GROUPS = J_CHUNK // J_GROUP

FLOPS = 2 * B * I * J * D
BYTES = 2 * I * J * K * D + 4 * B * I * D + 2 * B * I * D + 4 * B * J * D


def tile_primary_capsule_t_v_kernel(tc, X, weight, s, grad_out, out):
    nc = tc.nc
    s_rows = s.rearrange("(n p) i d -> n p i d", p=P)
    g_rows = grad_out.rearrange("(n p) i d -> n p i d", p=P)
    out_rows = out.rearrange("(n p) j d -> n p j d", p=P)
    w_rows = weight.rearrange("(c t p) j k d -> c p t j (k d)", t=PACK, p=P)

    with tc.tile_pool(name="sb", bufs=1) as sb, tc.psum_pool(name="ps", bufs=1) as ps, tc.manual_schedule():
        eps_col = sb.tile([P, 1], F32)
        nc.vector.memset(eps_col[:], EPS)
        one_col = sb.tile([P, 1], F32)
        nc.vector.memset(one_col[:], 1.0)
        ident = sb.tile([P, P], F32)
        make_identity(nc, ident[:])
        ident_bf = sb.tile([P, P], BF16)
        make_identity(nc, ident_bf[:])

        ds_codes = sb.tile([P, TOKEN_TILES, PASSES * D * P], U32, align_bytes=64)
        ds_scales = sb.tile([P, TOKEN_TILES, PASSES * D * P], U8, align_bytes=64)
        w_codes = sb.tile([P, W_CHUNKS, W_SLOT], U32, align_bytes=64)
        w_scales = sb.tile([P, W_CHUNKS, W_SLOT], U8, align_bytes=64)
        nc.vector.memset(w_codes[:, :, J_CHUNK : 2 * J_CHUNK].bitcast(I32), 0)
        nc.vector.memset(w_scales[:, :, J_CHUNK : 2 * J_CHUNK].bitcast(I32), 0)

        tokens = {}
        weights = {}
        banks = {}
        ready_tiles = []
        ready_chunks = []

        def load_tokens(n):
            s_sb = sb.tile([P, I, D], F32, tag="s", bufs=3)
            nc.sync.dma_start(out=s_sb[:], in_=s_rows[n])
            g_sb = sb.tile([P, I, D], BF16, tag="g", bufs=3)
            nc.sync.dma_start(out=g_sb[:], in_=g_rows[n])
            tokens[n] = {"s": s_sb, "g": g_sb}

        def load_weights(w):
            jc, c = divmod(w, PASSES)
            w_sb = sb.tile([P, PACK, J_CHUNK, K * D], BF16, tag="w", bufs=2)
            nc.sync.dma_start(out=w_sb[:], in_=w_rows[c][:, :, jc * J_CHUNK : (jc + 1) * J_CHUNK, :])
            weights[w] = {"w": w_sb}

        def token_squares(n):
            t = tokens[n]
            prod = sb.tile([P, 2, I, D], F32, tag="prod")
            nc.scalar.activation(out=prod[:, 0, :, :], in_=t["s"][:], func=ACT.Square)
            t["prod"] = prod

        def token_products(n):
            t = tokens[n]
            nc.vector.tensor_tensor(out=t["prod"][:, 1, :, :], in0=t["g"][:], in1=t["s"][:], op=ALU.mult)

        def token_sums(n):
            t = tokens[n]
            dots = sb.tile([P, 2, I], F32, tag="dots", bufs=2)
            nc.vector.tensor_tensor(
                out=dots[:], in0=t["prod"][:, :, :, 0], in1=t["prod"][:, :, :, 1], op=ALU.add
            )
            t["dots"] = dots

        def reciprocals(n):
            t = tokens[n]
            n2 = t["dots"][:, 0, :]
            r = sb.tile([P, I], F32, tag="r", bufs=2)
            a2 = sb.tile([P, I], F32, tag="a2", bufs=2)
            nc.scalar.activation(out=r[:], in_=n2, func=ACT.Abs_reciprocal_sqrt)
            nc.scalar.activation(out=a2[:], in_=n2, func=ACT.Square, bias=one_col[:])
            nc.scalar.activation(out=r[:], in_=r[:], func=ACT.Square)
            nc.scalar.activation(out=r[:], in_=r[:], func=ACT.Abs_reciprocal_sqrt)
            nc.scalar.activation(out=r[:], in_=r[:], func=ACT.Square, bias=eps_col[:])
            nc.scalar.activation(out=a2[:], in_=a2[:], func=ACT.Abs_reciprocal_sqrt, scale=0.25)
            nc.scalar.activation(out=r[:], in_=r[:], func=ACT.Abs_reciprocal_sqrt)
            t["r"] = r
            t["a2"] = a2

        def factor_parts(n):
            t = tokens[n]
            facs = sb.tile([P, 2, I], F32, tag="facs")
            nc.vector.tensor_tensor(out=facs[:, 0, :], in0=t["a2"][:], in1=t["r"][:], op=ALU.mult)
            nc.vector.scalar_tensor_tensor(
                out=t["r"][:], in0=t["r"][:], scalar=EPS, in1=t["a2"][:], op0=ALU.mult, op1=ALU.add
            )
            t["facs"] = facs

        def factor_c(n):
            t = tokens[n]
            nc.vector.scalar_tensor_tensor(
                out=t["facs"][:, 1, :], in0=t["r"][:], scalar=1.0, in1=t["facs"][:, 0, :],
                op0=ALU.subtract, op1=ALU.mult,
            )

        def factors(n):
            t = tokens[n]
            nc.vector.scalar_tensor_tensor(
                out=t["dots"][:], in0=t["dots"][:], scalar=0.5, in1=t["facs"][:], op0=ALU.mult, op1=ALU.mult
            )

        def term(n, which, name, source):
            t = tokens[n]
            planes = sb.tile([P, D, I], F32, tag=name)
            nc.vector.tensor_tensor(
                out=planes[:],
                in0=t["dots"][:, which, :].unsqueeze(1).to_broadcast([P, D, I]),
                in1=t[source][:].rearrange("p i d -> p d i"),
                op=ALU.mult,
            )
            t[name] = planes

        def turn_transposes(n):
            t = tokens[n]
            t["turned"] = []
            for c in range(PASSES):
                for d in range(D):
                    turned = ps.tile([P, PACK, P], F32, tag="tp", bufs=4)
                    for k in range(PACK):
                        i_cols = slice((c * PACK + k) * P, (c * PACK + k + 1) * P)
                        nc.tensor.matmul(
                            out=turned[:, k, :], lhsT=t["fg"][:, d, i_cols], rhs=ident[:],
                            is_transpose=True, start=True, stop=False,
                        )
                        nc.tensor.matmul(
                            out=turned[:, k, :], lhsT=t["hs"][:, d, i_cols], rhs=ident[:],
                            is_transpose=True, start=False, stop=True,
                        )
                    t["turned"].append(turned)

        def turn_copies(n):
            t = tokens[n]
            ds_bf = sb.tile([P, PASSES, D, P, PACK], BF16, tag="ds_bf", align_bytes=64)
            for c in range(PASSES):
                for d in range(D):
                    nc.scalar.copy(
                        out=ds_bf[:, c, d, :, :], in_=t["turned"][c * D + d][:].rearrange("p t b -> p b t")
                    )
            t["ds_bf"] = ds_bf

        def quantise_tokens(n):
            nc.vector.quantize_mx(
                out=ds_codes[:, n, :].bitcast(E5M2_X4),
                scales=ds_scales[:, n, :],
                in_=tokens[n]["ds_bf"][:].rearrange("p c d b t -> p (c d b t)"),
            )

        def first_j(w):
            return TENSOR_J if w == TENSOR_CHUNK else 0

        def weights_first_add(w):
            t = weights[w]
            half = sb.tile([P, J_CHUNK, PACK, 2 * D], F32, tag="half", bufs=2)
            nc.vector.tensor_tensor(
                out=half[:, first_j(w) :, :, :].rearrange("p j t e -> p t j e"),
                in0=t["w"][:, :, first_j(w) :, 0 : 2 * D],
                in1=t["w"][:, :, first_j(w) :, 2 * D : 4 * D],
                op=ALU.add,
            )
            ws_bf = sb.tile([P, D, J_CHUNK, PACK], BF16, tag="ws_bf", bufs=2, align_bytes=64)
            t["half"] = half
            t["ws_bf"] = ws_bf

        def weights_second_add(w):
            t = weights[w]
            nc.vector.tensor_tensor(
                out=t["ws_bf"][:, :, first_j(w) :, :].rearrange("p d j t -> p j t d"),
                in0=t["half"][:, first_j(w) :, :, 0:D],
                in1=t["half"][:, first_j(w) :, :, D : 2 * D],
                op=ALU.add,
            )

        def weights_first_add_planes(w):
            t = weights[w]
            planes = sb.tile([P, 2, PACK * J_CHUNK, D], F32, tag="half", bufs=2)
            rows = t["w"][:].rearrange("p t j e -> p (t j) e")
            nc.vector.tensor_tensor(
                out=planes[:].rearrange("p h x d -> p x h d"),
                in0=rows[:, :, 0 : 2 * D].rearrange("p x (h d) -> p x h d", d=D),
                in1=rows[:, :, 2 * D : 4 * D].rearrange("p x (h d) -> p x h d", d=D),
                op=ALU.add,
            )
            ws_bf = sb.tile([P, D, J_CHUNK, PACK], BF16, tag="ws_bf", bufs=2, align_bytes=64)
            t["planes"] = planes
            t["ws_bf"] = ws_bf

        def weights_turned_sum_note():
            pass

        def weights_forward(w):
            t = weights[w]
            t["forward"] = []
            for g in range(J_GROUPS):
                bank = ps.tile([P, PACK, P], F32, tag="tp", bufs=4)
                for k in range(PACK):
                    x0 = k * J_CHUNK + g * J_GROUP
                    for h in range(2):
                        nc.tensor.matmul(
                            out=bank[:, k, :],
                            lhsT=t["planes"][:, h, x0 : x0 + J_GROUP, :].rearrange("p x d -> p (x d)"),
                            rhs=ident[:], is_transpose=True, start=(h == 0), stop=(h == 1),
                        )
                t["forward"].append(bank)

        def weights_rounded(w):
            t = weights[w]
            t["rounded"] = []
            for g in range(J_GROUPS):
                mid = sb.tile([P, 2, P, 2], BF16, tag="mid", bufs=4, align_bytes=64)
                nc.scalar.copy(out=mid[:], in_=t["forward"][g][:].rearrange("q (u e) p -> q u p e", e=2))
                t["rounded"].append(mid)

        def weights_back(w):
            t = weights[w]
            t["back"] = []
            for pair in range(J_GROUPS // 2):
                bank = ps.tile([P, 2, 2, P], F32, tag="tp", bufs=4)
                for g in range(2):
                    words = t["rounded"][2 * pair + g][:].rearrange("q u p e -> q (u p e)").bitcast(F32)
                    for u in range(2):
                        nc.tensor.transpose(
                            out=bank[:, u, g, :], in_=words[:, u * P : (u + 1) * P], identity=ident[:]
                        )
                t["back"].append(bank)

        def weights_placed(w):
            t = weights[w]
            for pair in range(J_GROUPS // 2):
                j_cols = slice(pair * 2 * J_GROUP, (pair + 1) * 2 * J_GROUP)
                nc.scalar.copy(
                    out=t["ws_bf"][:].bitcast(F32)[:, :, j_cols, :],
                    in_=t["back"][pair][:].rearrange("p u g (j d) -> p d (g j) u", d=D),
                )

        def weights_tensor_sum(w):
            t = weights[w]
            for j0 in range(0, first_j(w), TENSOR_J_GROUP):
                j_cols = slice(j0, j0 + TENSOR_J_GROUP)
                summed = ps.tile([P, PACK, TENSOR_J_GROUP, D], F32, tag="tp", bufs=4)
                for k in range(K):
                    nc.tensor.matmul(
                        out=summed[:], lhsT=ident_bf[:], rhs=t["w"][:, :, j_cols, k * D : (k + 1) * D],
                        start=(k == 0), stop=(k == K - 1),
                    )
                nc.scalar.copy(out=t["ws_bf"][:, :, j_cols, :], in_=summed[:].rearrange("p t j d -> p d j t"))

        def weights_quantise(w, d):
            cols = slice(2 * d * J_CHUNK, (2 * d + 1) * J_CHUNK)
            nc.vector.quantize_mx(
                out=w_codes[:, w, cols].bitcast(E4M3_X4),
                scales=w_scales[:, w, cols],
                in_=weights[w]["ws_bf"][:, d, :, :].rearrange("p j t -> p (j t)"),
            )

        def multiply(w, tiles):
            jc, c = divmod(w, PASSES)
            for n in tiles:
                if c == 0:
                    bank = ps.tile([P, D, J_CHUNK], F32, tag="bank", bufs=4)
                    banks[n] = bank
                for d in range(D):
                    ds_cols = slice((c * D + d) * P, (c * D + d + 1) * P)
                    w_cols = slice(d * J_CHUNK, (d + 2) * J_CHUNK)
                    nc.tensor.matmul_mx(
                        out=banks[n][:].rearrange("p d j -> p (d j)"),
                        lhsT=ds_codes[:, n, ds_cols].bitcast(E5M2_X4),
                        lhsT_scale=ds_scales[:, n, ds_cols],
                        rhs=w_codes[:, w, w_cols].bitcast(E4M3_X4),
                        rhs_scale=w_scales[:, w, w_cols],
                        start=(c == 0 and d == 0),
                        stop=(c == PASSES - 1 and d == D - 1),
                    )
            if c == PASSES - 1:
                for n in tiles:
                    result = sb.tile([P, J_CHUNK, D], F32, tag="result", bufs=4)
                    out_cols = out_rows[n][:, jc * J_CHUNK : (jc + 1) * J_CHUNK, :]
                    if jc == J_CHUNKS - 1 and n % 2 == 1:
                        nc.vector.tensor_copy(out=result[:], in_=banks[n][:].rearrange("p d j -> p j d"))
                        nc.sync.dma_start(out=out_cols, in_=result[:])
                    else:
                        nc.scalar.copy(out=result[:], in_=banks[n][:].rearrange("p d j -> p j d"))
                        nc.scalar.dma_start(out=out_cols, in_=result[:])

        def chunk_ready(w):
            multiply(w, ready_tiles)
            ready_chunks.append(w)

        def tile_ready(n):
            for w in ready_chunks:
                multiply(w, [n])
            ready_tiles.append(n)

        load_tokens(0)
        load_weights(0)
        load_tokens(1)
        load_weights(1)
        load_tokens(2)
        token_squares(0)
        token_products(0)
        token_sums(0)
        reciprocals(0)
        token_squares(1)
        for w in range(LEAD):
            weights_first_add_planes(w)
            load_weights(w + 2)
            weights_forward(w)
            weights_rounded(w)
            weights_back(w)
            weights_placed(w)
        token_products(1)
        for n in range(TOKEN_TILES):
            w = LEAD + n
            if n >= 1:
                turn_copies(n - 1)
            if n == 0:
                weights_first_add_planes(w)
                load_weights(w + 2)
                weights_forward(w)
            if n + 1 < TOKEN_TILES:
                token_sums(n + 1)
                reciprocals(n + 1)
            factor_parts(n)
            if n + 2 < TOKEN_TILES:
                token_squares(n + 2)
            if n >= 1:
                weights_first_add_planes(w)
                load_weights(w + 2)
                weights_forward(w)
            factor_c(n)
            weights_quantise(w - 1, 0)
            factors(n)
            weights_quantise(w - 1, 1)
            weights_rounded(w)
            weights_back(w)
            weights_placed(w)
            chunk_ready(w - 1)
            term(n, 0, "fg", "g")
            if n >= 1:
                quantise_tokens(n - 1)
                tile_ready(n - 1)
            if n == TOKEN_TILES - 1:
                weights_first_add(TENSOR_CHUNK)
                load_weights(TENSOR_CHUNK + 2)
                weights_tensor_sum(TENSOR_CHUNK)
            term(n, 1, "hs", "s")
            turn_transposes(n)
            if n + 2 < TOKEN_TILES:
                token_products(n + 2)
            if n + 3 < TOKEN_TILES:
                load_tokens(n + 3)
        turn_copies(TOKEN_TILES - 1)
        for w in range(ROUND_CHUNKS, W_CHUNKS):
            weights_second_add(w)
            if w == ROUND_CHUNKS:
                weights_quantise(w - 1, 0)
                weights_quantise(w - 1, 1)
                chunk_ready(w - 1)
            if w == ROUND_CHUNKS + 1:
                quantise_tokens(TOKEN_TILES - 1)
                tile_ready(TOKEN_TILES - 1)
            if w + 1 < W_CHUNKS:
                weights_first_add(w + 1)
            weights_quantise(w, 0)
            weights_quantise(w, 1)
            chunk_ready(w)
